import numpy as np
import ml_dtypes


def mxq(x, axis, fmt="e4m3"):
    dtype, down = {"e4m3": (ml_dtypes.float8_e4m3fn, 7), "e5m2": (ml_dtypes.float8_e5m2, 14)}[fmt]
    v = np.moveaxis(np.asarray(x, np.float32).astype(ml_dtypes.bfloat16).astype(np.float64), axis, -1)
    blocks = v.reshape(v.shape[:-1] + (-1, 32))
    amax = np.abs(blocks).max(-1, keepdims=True)
    byte = np.maximum(np.where(amax > 0, np.frexp(amax)[1] - 1 + 127, 0) - down, 1)
    scale = np.exp2(byte - 127.0)
    codes = (blocks / scale).astype(np.float32).astype(dtype).astype(np.float64)
    return np.moveaxis((codes * scale).reshape(v.shape), -1, axis)


WIDE = False


def mx_kscale(k):
    if not WIDE:
        return np.ones(k)
    levels = np.array([10, -10, 5, -5, 0])
    a = np.random.permutation(np.resize(levels, k // 512 * 4)).reshape(k // 512, 4)
    idx = np.arange(k)
    return np.exp2(a[idx // 512, idx % 128 // 32])


BF16 = ml_dtypes.bfloat16


def bf(x):
    return np.asarray(x, np.float32).astype(BF16)


def f64(x):
    return np.asarray(x).astype(np.float64)


TOKENS, D_MODEL, D_FF = 512, 1024, 4096


def gelu_tanh(v):
    return 0.5 * v * (1.0 + np.tanh(np.sqrt(2.0 / np.pi) * (v + 0.044715 * v**3)))


def setup_inputs():
    s = mx_kscale(D_MODEL)
    return {"x": bf(np.random.standard_normal((TOKENS, D_MODEL)) * s),
            "w1_fp8": bf(np.random.standard_normal((D_MODEL, D_FF)) * 0.03 / s[:, None]),
            "b1": bf(np.random.standard_normal(D_FF) * 0.2),
            "w2_fp8": bf(np.random.standard_normal((D_FF, D_MODEL)) * 0.03),
            "b2": bf(np.random.standard_normal(D_MODEL) * 0.3)}


def reference(x, w1_fp8, b1, w2_fp8, b2):
    h = gelu_tanh((mxq(f64(x), 1, "e4m3") @ mxq(f64(w1_fp8), 0, "e4m3")) + f64(b1))
    return (mxq(h, 1, "e4m3") @ mxq(f64(w2_fp8), 0, "e4m3")) + f64(b2)

@@ -1,0 +1,278 @@
+from contextlib import ExitStack
+
+import concourse.mybir as mybir
+from concourse.masks import make_identity
+
+FLOPS = 2 * 512 * 1024 * 4096 * 2
+
+F32 = mybir.dt.float32
+BF16 = mybir.dt.bfloat16
+U32 = mybir.dt.uint32
+U8 = mybir.dt.uint8
+FP8X4 = mybir.dt.float8_e4m3fn_x4
+ACT = mybir.ActivationFunctionType
+ALU = mybir.AluOpType
+
+P = 128
+N_UNITS = 16
+
+
+def scalar_columns(j):
+    if j < 2:
+        return 288
+    if j < 10:
+        return 216
+    return 288
+
+
+def tile_fp8modelwrapper_kernel(tc, x, w1_fp8, b1, w2_fp8, b2, out):
+    nc = tc.nc
+    with ExitStack() as ctx:
+        const = ctx.enter_context(tc.tile_pool(name="const", bufs=1))
+        rawp = ctx.enter_context(tc.tile_pool(name="rawp", bufs=6))
+        grpp = ctx.enter_context(tc.tile_pool(name="grpp", bufs=3))
+        codep = ctx.enter_context(tc.tile_pool(name="codep", bufs=3))
+        hpool = ctx.enter_context(tc.tile_pool(name="hpool", bufs=2))
+        outp = ctx.enter_context(tc.tile_pool(name="outp", bufs=4))
+        psum = ctx.enter_context(tc.psum_pool(name="psum", bufs=1))
+        ctx.enter_context(tc.manual_schedule())
+
+        scr_in = const.tile([P, 1], F32, name="scr_in")
+        scr_out = const.tile([P, 1], F32, name="scr_out")
+        b1rows = const.tile([P, P], BF16, name="b1rows")
+        nc.vector.memset(b1rows[:], 0.0)
+        nc.vector.memset(scr_in[:], 0.0)
+        nc.scalar.dma_start(out=b1rows[0:32, :], in_=b1.rearrange("(r c) -> r c", c=P))
+        nc.scalar.activation(out=scr_out[:], in_=scr_in[:], func=ACT.Gelu_apprx_tanh)
+        ident = const.tile([P, P], F32, name="ident")
+        make_identity(nc, ident[:])
+
+        raw = {}
+        w1v = w1_fp8.rearrange("(g u q e) f -> g u q e f", g=2, u=2, q=P, e=2)
+        w2v = w2_fp8.rearrange("(c s p) n -> c p s n", c=4, s=8, p=P)
+
+        def new_raw(i):
+            raw[i] = rawp.tile([P, 8, 1024], BF16, name="raw%d" % i, tag="raw")
+
+        def load_w1(i, g, c0, c1):
+            for u in range(2):
+                s = 4 * g + 2 * u
+                nc.sync.dma_start(
+                    out=raw[i][:, s : s + 2, c0:c1],
+                    in_=w1v[g, u][:, :, 1024 * i + c0 : 1024 * i + c1],
+                )
+
+        def load_w2(c):
+            new_raw(4 + c)
+            for hs in range(2):
+                nc.sync.dma_start(
+                    out=raw[4 + c][:, 4 * hs : 4 * hs + 4, :], in_=w2v[c][:, 4 * hs : 4 * hs + 4, :]
+                )
+
+        x_sb = const.tile([P, 4096], BF16, name="x_sb")
+        x_sb3 = x_sb[:].rearrange("p (a k) -> p a k", a=4)
+        xv = x.rearrange("(a p) k -> p a k", p=P)
+
+        new_raw(0)
+        load_w1(0, 0, 0, 512)
+        nc.sync.dma_start(out=x_sb3[:, 0:2, :], in_=xv[:, 0:2, :])
+        nc.sync.dma_start(out=x_sb3[:, 2:4, :], in_=xv[:, 2:4, :])
+        load_w1(0, 1, 0, 512)
+        load_w1(0, 0, 512, 1024)
+        load_w1(0, 1, 512, 1024)
+        for i in range(1, 4):
+            new_raw(i)
+            load_w1(i, 0, 0, 1024)
+            load_w1(i, 1, 0, 1024)
+        load_w2(0)
+        load_w2(1)
+
+        grp = {}
+        wcode = {}
+        wscale = {}
+
+        def unit_src(j):
+            if j < 8:
+                return raw[j // 2], 512 * (j % 2)
+            return raw[4 + (j - 8) % 4], 512 * ((j - 8) // 4)
+
+        def regroup(copy, dst, src):
+            copy(
+                out=dst.rearrange("p (c i) t -> p c t i", i=4),
+                in_=src.rearrange("p t (c i) -> p c t i", i=4),
+            )
+
+        def new_grp(j):
+            grp[j] = grpp.tile([P, 2, 512, 4], BF16, name="grp%d" % j, tag="grp", align_bytes=64)
+
+        def regroup_scalar(j, g):
+            src, base = unit_src(j)
+            cs = scalar_columns(j)
+            regroup(nc.scalar.copy, grp[j][:, g, 0:cs, :], src[:, 4 * g : 4 * g + 4, base : base + cs])
+
+        def regroup_vector(j, g):
+            src, base = unit_src(j)
+            cs = scalar_columns(j)
+            regroup(
+                nc.vector.tensor_copy,
+                grp[j][:, g, cs:512, :],
+                src[:, 4 * g : 4 * g + 4, base + cs : base + 512],
+            )
+
+        def quantise_unit(j):
+            wcode[j] = codep.tile([P, 1024], U32, name="wc%d" % j, tag="wc", align_bytes=64)
+            wscale[j] = codep.tile([P, 1024], U8, name="ws%d" % j, tag="ws", align_bytes=64)
+            nc.vector.quantize_mx(
+                out=wcode[j][:].bitcast(FP8X4),
+                scales=wscale[j][:],
+                in_=grp[j][:].rearrange("p g c t -> p (g c t)"),
+            )
+
+        new_grp(0)
+        regroup_scalar(0, 0)
+        regroup_vector(0, 0)
+
+        b1f = const.tile([P, P], F32, name="b1f")
+        nc.gpsimd.tensor_copy(out=b1f[:], in_=b1rows[:])
+        b1ps = psum.tile([P, 512], F32, name="b1ps", tag="B0")
+        nc.tensor.transpose(b1ps[:, 0:P], b1f[:], ident[:])
+        b1col = const.tile([P, 32], F32, name="b1col")
+
+        xw = x_sb[:].bitcast(F32)
+        xg = const.tile([P, 4096], BF16, name="xg", align_bytes=64)
+        xgw = xg[:].bitcast(F32).rearrange("p (g w u) -> p g w u", g=2, u=2)
+        xt = {}
+        for h in range(2):
+            for g in range(2):
+                xt[(g, h)] = psum.tile([P, 512], F32, name="xt%d%d" % (g, h), tag="A%d" % (2 * h + g))
+                for u in range(2):
+                    for a2 in range(2):
+                        a = 2 * h + a2
+                        col = 512 * a + 256 * g + 128 * u
+                        nc.tensor.transpose(
+                            xt[(g, h)][:, 256 * u + 128 * a2 : 256 * u + 128 * a2 + 128],
+                            xw[:, col : col + 128],
+                            ident[:],
+                        )
+        nc.vector.tensor_copy(out=b1col[:], in_=b1ps[:, 0:32])
+        for h in range(2):
+            for g in range(2):
+                copy = nc.scalar.copy if g == 0 else nc.vector.tensor_copy
+                copy(
+                    out=xgw[:, g, 256 * h : 256 * h + 256, :],
+                    in_=xt[(g, h)][:].rearrange("p (u w) -> p w u", u=2),
+                )
+        regroup_scalar(0, 1)
+        regroup_vector(0, 1)
+        new_grp(1)
+        regroup_scalar(1, 0)
+        regroup_scalar(1, 1)
+
+        xcode = const.tile([P, 1024], U32, name="xcode", align_bytes=64)
+        xscale = const.tile([P, 1024], U8, name="xscale", align_bytes=64)
+        nc.vector.quantize_mx(out=xcode[:].bitcast(FP8X4), scales=xscale[:], in_=xg[:])
+
+        hplane = {}
+        hgrp = {}
+        hcode = {}
+        hscale = {}
+        pm = {}
+        acc = {}
+        b2bc = const.tile([P, 1024], BF16, name="b2bc")
+
+        def first_matmul(j):
+            for m in range(4):
+                pm[(j, m)] = psum.tile([P, 512], F32, name="pm%d_%d" % (j, m), tag="B%d" % m)
+                for g in range(2):
+                    cols = slice(512 * g + 128 * m, 512 * g + 128 * m + 128)
+                    nc.tensor.matmul_mx(
+                        out=pm[(j, m)][:],
+                        lhsT=wcode[j][:, cols].bitcast(FP8X4),
+                        lhsT_scale=wscale[j][:, cols],
+                        rhs=xcode[:, 512 * g : 512 * g + 512].bitcast(FP8X4),
+                        rhs_scale=xscale[:, 512 * g : 512 * g + 512],
+                        start=(g == 0),
+                        stop=(g == 1),
+                    )
+
+        def gelu(j):
+            hplane[j] = hpool.tile([P, 4, 512], BF16, name="hp%d" % j, tag="hp")
+            for m in range(4):
+                nc.scalar.activation(
+                    out=hplane[j][:, m, :],
+                    in_=pm[(j, m)][:],
+                    func=ACT.Gelu_apprx_tanh,
+                    bias=b1col[:, 4 * j + m : 4 * j + m + 1],
+                    scale=1.0,
+                )
+
+        def regroup_h(j):
+            hgrp[j] = hpool.tile([P, 512, 4], BF16, name="hg%d" % j, tag="hg", align_bytes=64)
+            regroup(nc.vector.tensor_copy, hgrp[j][:], hplane[j][:])
+
+        def quantise_h(j):
+            hcode[j] = const.tile([P, 512], U32, name="hc%d" % j, align_bytes=64)
+            hscale[j] = const.tile([P, 512], U8, name="hs%d" % j, align_bytes=64)
+            nc.vector.quantize_mx(
+                out=hcode[j][:].bitcast(FP8X4),
+                scales=hscale[j][:],
+                in_=hgrp[j][:].rearrange("p w t -> p (w t)"),
+            )
+
+        def second_matmul(j):
+            c = (j - 8) % 4
+            half = (j - 8) // 4
+            for gi in range(2):
+                g = 2 * c + gi
+                for a in range(4):
+                    if g == 0:
+                        acc[(half, a)] = psum.tile(
+                            [P, 512], F32, name="acc%d_%d" % (half, a), tag="%s%d" % ("AB"[half], a)
+                        )
+                    nc.tensor.matmul_mx(
+                        out=acc[(half, a)][:],
+                        lhsT=hcode[g][:, 128 * a : 128 * a + 128].bitcast(FP8X4),
+                        lhsT_scale=hscale[g][:, 128 * a : 128 * a + 128],
+                        rhs=wcode[j][:, 512 * gi : 512 * gi + 512].bitcast(FP8X4),
+                        rhs_scale=wscale[j][:, 512 * gi : 512 * gi + 512],
+                        start=(g == 0),
+                        stop=(g == 7),
+                    )
+
+        def finish(half):
+            for a in range(4):
+                o = outp.tile([P, 512], F32, name="o%d_%d" % (half, a), tag="osb")
+                nc.vector.tensor_tensor(
+                    out=o[:], in0=acc[(half, a)][:], in1=b2bc[:, 512 * half : 512 * half + 512], op=ALU.add
+                )
+                nc.sync.dma_start(
+                    out=out[128 * a : 128 * a + 128, 512 * half : 512 * half + 512], in_=o[:]
+                )
+
+        for j in range(N_UNITS):
+            quantise_unit(j)
+            if j < 8:
+                first_matmul(j)
+            else:
+                second_matmul(j)
+            if j == 12:
+                finish(0)
+            if 1 <= j <= 8:
+                regroup_h(j - 1)
+            if j < 8:
+                gelu(j)
+            if j + 2 < N_UNITS:
+                new_grp(j + 2)
+                regroup_scalar(j + 2, 0)
+                regroup_scalar(j + 2, 1)
+            if j + 1 < N_UNITS:
+                regroup_vector(j + 1, 0)
+                regroup_vector(j + 1, 1)
+            if 1 <= j <= 8:
+                quantise_h(j - 1)
+            if j == 0:
+                load_w2(2)
+            if j == 2:
+                load_w2(3)
+                nc.sync.dma_start(out=b2bc[:], in_=b2.partition_broadcast(P))
+        finish(1)

@@ -15,21 +15,15 @@ ALU = mybir.AluOpType
 
 P = 128
 N_UNITS = 16
-
-
-def scalar_columns(j):
-    if j < 2:
-        return 288
-    if j < 10:
-        return 216
-    return 288
+SCALAR_COLUMNS = [288] * 2 + [216] * 8 + [264] * 4 + [408] * 2
+FINISH_0 = {13: (0, 1), 14: (2, 3)}
 
 
 def tile_fp8modelwrapper_kernel(tc, x, w1_fp8, b1, w2_fp8, b2, out):
     nc = tc.nc
     with ExitStack() as ctx:
         const = ctx.enter_context(tc.tile_pool(name="const", bufs=1))
-        rawp = ctx.enter_context(tc.tile_pool(name="rawp", bufs=6))
+        rawp = ctx.enter_context(tc.tile_pool(name="rawp", bufs=5))
         grpp = ctx.enter_context(tc.tile_pool(name="grpp", bufs=3))
         codep = ctx.enter_context(tc.tile_pool(name="codep", bufs=3))
         hpool = ctx.enter_context(tc.tile_pool(name="hpool", bufs=2))
@@ -47,54 +41,53 @@ def tile_fp8modelwrapper_kernel(tc, x, w1_fp8, b1, w2_fp8, b2, out):
         ident = const.tile([P, P], F32, name="ident")
         make_identity(nc, ident[:])
 
-        raw = {}
         w1v = w1_fp8.rearrange("(g u q e) f -> g u q e f", g=2, u=2, q=P, e=2)
         w2v = w2_fp8.rearrange("(c s p) n -> c p s n", c=4, s=8, p=P)
+        source = {}
 
-        def new_raw(i):
-            raw[i] = rawp.tile([P, 8, 1024], BF16, name="raw%d" % i, tag="raw")
+        def load_w1_small(j):
+            for g in range(2):
+                t = const.tile([P, 4, 512], BF16, name="rs%d_%d" % (j, g))
+                for u in range(2):
+                    nc.sync.dma_start(
+                        out=t[:, 2 * u : 2 * u + 2, :], in_=w1v[g, u][:, :, 512 * j : 512 * j + 512]
+                    )
+                source[(j, g)] = t[:]
 
-        def load_w1(i, g, c0, c1):
-            for u in range(2):
-                s = 4 * g + 2 * u
-                nc.sync.dma_start(
-                    out=raw[i][:, s : s + 2, c0:c1],
-                    in_=w1v[g, u][:, :, 1024 * i + c0 : 1024 * i + c1],
-                )
+        def load_w1_chunk(i):
+            t = rawp.tile([P, 8, 1024], BF16, name="raw1_%d" % i, tag="raw")
+            for g in range(2):
+                for u in range(2):
+                    s = 4 * g + 2 * u
+                    nc.sync.dma_start(
+                        out=t[:, s : s + 2, :], in_=w1v[g, u][:, :, 1024 * i : 1024 * i + 1024]
+                    )
+                for hf in range(2):
+                    source[(2 * i + hf, g)] = t[:, 4 * g : 4 * g + 4, 512 * hf : 512 * hf + 512]
 
-        def load_w2(c):
-            new_raw(4 + c)
-            for hs in range(2):
-                nc.sync.dma_start(
-                    out=raw[4 + c][:, 4 * hs : 4 * hs + 4, :], in_=w2v[c][:, 4 * hs : 4 * hs + 4, :]
-                )
+        def load_w2_chunk(c):
+            t = rawp.tile([P, 8, 1024], BF16, name="raw2_%d" % c, tag="raw")
+            for g in range(2):
+                nc.sync.dma_start(out=t[:, 4 * g : 4 * g + 4, :], in_=w2v[c][:, 4 * g : 4 * g + 4, :])
+                for half in range(2):
+                    source[(8 + 4 * half + c, g)] = t[:, 4 * g : 4 * g + 4, 512 * half : 512 * half + 512]
 
         x_sb = const.tile([P, 4096], BF16, name="x_sb")
         x_sb3 = x_sb[:].rearrange("p (a k) -> p a k", a=4)
         xv = x.rearrange("(a p) k -> p a k", p=P)
-
-        new_raw(0)
-        load_w1(0, 0, 0, 512)
         nc.sync.dma_start(out=x_sb3[:, 0:2, :], in_=xv[:, 0:2, :])
         nc.sync.dma_start(out=x_sb3[:, 2:4, :], in_=xv[:, 2:4, :])
-        load_w1(0, 1, 0, 512)
-        load_w1(0, 0, 512, 1024)
-        load_w1(0, 1, 512, 1024)
-        for i in range(1, 4):
-            new_raw(i)
-            load_w1(i, 0, 0, 1024)
-            load_w1(i, 1, 0, 1024)
-        load_w2(0)
-        load_w2(1)
+        for j in range(4):
+            load_w1_small(j)
+        load_w1_chunk(2)
+        load_w1_chunk(3)
+        load_w2_chunk(0)
+        load_w2_chunk(1)
+        load_w2_chunk(2)
 
         grp = {}
         wcode = {}
         wscale = {}
-
-        def unit_src(j):
-            if j < 8:
-                return raw[j // 2], 512 * (j % 2)
-            return raw[4 + (j - 8) % 4], 512 * ((j - 8) // 4)
 
         def regroup(copy, dst, src):
             copy(
@@ -102,41 +95,27 @@ def tile_fp8modelwrapper_kernel(tc, x, w1_fp8, b1, w2_fp8, b2, out):
                 in_=src.rearrange("p t (c i) -> p c t i", i=4),
             )
 
-        def new_grp(j):
-            grp[j] = grpp.tile([P, 2, 512, 4], BF16, name="grp%d" % j, tag="grp", align_bytes=64)
-
         def regroup_scalar(j, g):
-            src, base = unit_src(j)
-            cs = scalar_columns(j)
-            regroup(nc.scalar.copy, grp[j][:, g, 0:cs, :], src[:, 4 * g : 4 * g + 4, base : base + cs])
+            if g == 0:
+                grp[j] = grpp.tile([P, 2, 512, 4], BF16, name="grp%d" % j, tag="grp", align_bytes=64)
+            cs = SCALAR_COLUMNS[j]
+            regroup(nc.scalar.copy, grp[j][:, g, 0:cs, :], source[(j, g)][:, :, 0:cs])
 
         def regroup_vector(j, g):
-            src, base = unit_src(j)
-            cs = scalar_columns(j)
-            regroup(
-                nc.vector.tensor_copy,
-                grp[j][:, g, cs:512, :],
-                src[:, 4 * g : 4 * g + 4, base + cs : base + 512],
-            )
+            cs = SCALAR_COLUMNS[j]
+            regroup(nc.vector.tensor_copy, grp[j][:, g, cs:512, :], source[(j, g)][:, :, cs:512])
 
-        def quantise_unit(j):
-            wcode[j] = codep.tile([P, 1024], U32, name="wc%d" % j, tag="wc", align_bytes=64)
-            wscale[j] = codep.tile([P, 1024], U8, name="ws%d" % j, tag="ws", align_bytes=64)
+        def quantise_unit(j, parts):
+            if 0 in parts:
+                wcode[j] = codep.tile([P, 1024], U32, name="wc%d" % j, tag="wc", align_bytes=64)
+                wscale[j] = codep.tile([P, 1024], U8, name="ws%d" % j, tag="ws", align_bytes=64)
+            lo = 512 * parts[0]
+            hi = 512 * parts[-1] + 512
             nc.vector.quantize_mx(
-                out=wcode[j][:].bitcast(FP8X4),
-                scales=wscale[j][:],
-                in_=grp[j][:].rearrange("p g c t -> p (g c t)"),
+                out=wcode[j][:, lo:hi].bitcast(FP8X4),
+                scales=wscale[j][:, lo:hi],
+                in_=grp[j][:, parts[0] : parts[-1] + 1, :, :].rearrange("p g c t -> p (g c t)"),
             )
-
-        new_grp(0)
-        regroup_scalar(0, 0)
-        regroup_vector(0, 0)
-
-        b1f = const.tile([P, P], F32, name="b1f")
-        nc.gpsimd.tensor_copy(out=b1f[:], in_=b1rows[:])
-        b1ps = psum.tile([P, 512], F32, name="b1ps", tag="B0")
-        nc.tensor.transpose(b1ps[:, 0:P], b1f[:], ident[:])
-        b1col = const.tile([P, 32], F32, name="b1col")
 
         xw = x_sb[:].bitcast(F32)
         xg = const.tile([P, 4096], BF16, name="xg", align_bytes=64)
@@ -154,7 +133,12 @@ def tile_fp8modelwrapper_kernel(tc, x, w1_fp8, b1, w2_fp8, b2, out):
                             xw[:, col : col + 128],
                             ident[:],
                         )
-        nc.vector.tensor_copy(out=b1col[:], in_=b1ps[:, 0:32])
+        b1f = const.tile([P, P], F32, name="b1f")
+        nc.gpsimd.tensor_copy(out=b1f[:], in_=b1rows[:])
+        b1ps = psum.tile([P, 512], F32, name="b1ps", tag="B0")
+        nc.tensor.transpose(b1ps[:, 0:P], b1f[:], ident[:])
+        b1col = const.tile([P, 32], F32, name="b1col")
+
         for h in range(2):
             for g in range(2):
                 copy = nc.scalar.copy if g == 0 else nc.vector.tensor_copy
@@ -162,15 +146,15 @@ def tile_fp8modelwrapper_kernel(tc, x, w1_fp8, b1, w2_fp8, b2, out):
                     out=xgw[:, g, 256 * h : 256 * h + 256, :],
                     in_=xt[(g, h)][:].rearrange("p (u w) -> p w u", u=2),
                 )
-        regroup_scalar(0, 1)
-        regroup_vector(0, 1)
-        new_grp(1)
-        regroup_scalar(1, 0)
-        regroup_scalar(1, 1)
-
         xcode = const.tile([P, 1024], U32, name="xcode", align_bytes=64)
         xscale = const.tile([P, 1024], U8, name="xscale", align_bytes=64)
         nc.vector.quantize_mx(out=xcode[:].bitcast(FP8X4), scales=xscale[:], in_=xg[:])
+        nc.vector.tensor_copy(out=b1col[:], in_=b1ps[:, 0:32])
+        for g in range(2):
+            regroup_scalar(0, g)
+            regroup_vector(0, g)
+        for g in range(2):
+            regroup_scalar(1, g)
 
         hplane = {}
         hgrp = {}
@@ -182,7 +166,7 @@ def tile_fp8modelwrapper_kernel(tc, x, w1_fp8, b1, w2_fp8, b2, out):
 
         def first_matmul(j):
             for m in range(4):
-                pm[(j, m)] = psum.tile([P, 512], F32, name="pm%d_%d" % (j, m), tag="B%d" % m)
+                pm[(j, m)] = psum.tile([P, 512], F32, name="pm%d_%d" % (j, m), tag="%s%d" % ("AB"[j % 2], m))
                 for g in range(2):
                     cols = slice(512 * g + 128 * m, 512 * g + 128 * m + 128)
                     nc.tensor.matmul_mx(
@@ -219,28 +203,27 @@ def tile_fp8modelwrapper_kernel(tc, x, w1_fp8, b1, w2_fp8, b2, out):
                 in_=hgrp[j][:].rearrange("p w t -> p (w t)"),
             )
 
-        def second_matmul(j):
+        def second_matmul(j, gi):
             c = (j - 8) % 4
             half = (j - 8) // 4
-            for gi in range(2):
-                g = 2 * c + gi
-                for a in range(4):
-                    if g == 0:
-                        acc[(half, a)] = psum.tile(
-                            [P, 512], F32, name="acc%d_%d" % (half, a), tag="%s%d" % ("AB"[half], a)
-                        )
-                    nc.tensor.matmul_mx(
-                        out=acc[(half, a)][:],
-                        lhsT=hcode[g][:, 128 * a : 128 * a + 128].bitcast(FP8X4),
-                        lhsT_scale=hscale[g][:, 128 * a : 128 * a + 128],
-                        rhs=wcode[j][:, 512 * gi : 512 * gi + 512].bitcast(FP8X4),
-                        rhs_scale=wscale[j][:, 512 * gi : 512 * gi + 512],
-                        start=(g == 0),
-                        stop=(g == 7),
-                    )
-
-        def finish(half):
+            g = 2 * c + gi
             for a in range(4):
+                if g == 0:
+                    acc[(half, a)] = psum.tile(
+                        [P, 512], F32, name="acc%d_%d" % (half, a), tag="%s%d" % ("AB"[half], a)
+                    )
+                nc.tensor.matmul_mx(
+                    out=acc[(half, a)][:],
+                    lhsT=hcode[g][:, 128 * a : 128 * a + 128].bitcast(FP8X4),
+                    lhsT_scale=hscale[g][:, 128 * a : 128 * a + 128],
+                    rhs=wcode[j][:, 512 * gi : 512 * gi + 512].bitcast(FP8X4),
+                    rhs_scale=wscale[j][:, 512 * gi : 512 * gi + 512],
+                    start=(g == 0),
+                    stop=(g == 7),
+                )
+
+        def finish(half, tiles):
+            for a in tiles:
                 o = outp.tile([P, 512], F32, name="o%d_%d" % (half, a), tag="osb")
                 nc.vector.tensor_tensor(
                     out=o[:], in0=acc[(half, a)][:], in1=b2bc[:, 512 * half : 512 * half + 512], op=ALU.add
@@ -250,29 +233,33 @@ def tile_fp8modelwrapper_kernel(tc, x, w1_fp8, b1, w2_fp8, b2, out):
                 )
 
         for j in range(N_UNITS):
-            quantise_unit(j)
-            if j < 8:
-                first_matmul(j)
+            if j == N_UNITS - 1:
+                for gi in range(2):
+                    quantise_unit(j, (gi,))
+                    second_matmul(j, gi)
             else:
-                second_matmul(j)
-            if j == 12:
-                finish(0)
-            if 1 <= j <= 8:
-                regroup_h(j - 1)
-            if j < 8:
-                gelu(j)
+                quantise_unit(j, (0, 1))
+                if j < 8:
+                    first_matmul(j)
+                else:
+                    second_matmul(j, 0)
+                    second_matmul(j, 1)
+            if j in FINISH_0:
+                finish(0, FINISH_0[j])
+            if j + 1 < N_UNITS:
+                regroup_vector(j + 1, 0)
+            if 0 <= j - 2 < 8:
+                regroup_h(j - 2)
+            if 0 <= j - 1 < 8:
+                gelu(j - 1)
             if j + 2 < N_UNITS:
-                new_grp(j + 2)
                 regroup_scalar(j + 2, 0)
                 regroup_scalar(j + 2, 1)
             if j + 1 < N_UNITS:
-                regroup_vector(j + 1, 0)
                 regroup_vector(j + 1, 1)
-            if 1 <= j <= 8:
-                quantise_h(j - 1)
-            if j == 0:
-                load_w2(2)
-            if j == 2:
-                load_w2(3)
+            if 0 <= j - 2 < 8:
+                quantise_h(j - 2)
+            if j == 4:
+                load_w2_chunk(3)
                 nc.sync.dma_start(out=b2bc[:], in_=b2.partition_broadcast(P))
-        finish(1)
+        finish(1, (0, 1, 2, 3))

@@ -15,7 +15,8 @@ ALU = mybir.AluOpType
 
 P = 128
 N_UNITS = 16
-SCALAR_COLUMNS = [288] * 2 + [216] * 8 + [264] * 4 + [408] * 2
+TENSOR_COLUMNS = [0] * 3 + [256] * 7 + [0] * 6
+SCALAR_END = [320] * 2 + [216] + [304] * 7 + [264] * 4 + [456] * 2
 FINISH_0 = {13: (0, 1), 14: (2, 3)}
 
 
@@ -31,6 +32,9 @@ def tile_fp8modelwrapper_kernel(tc, x, w1_fp8, b1, w2_fp8, b2, out):
         psum = ctx.enter_context(tc.psum_pool(name="psum", bufs=1))
         ctx.enter_context(tc.manual_schedule())
 
+        def bank(name, k):
+            return psum.tile([P, 512], F32, name=name, tag="T%d" % k)
+
         scr_in = const.tile([P, 1], F32, name="scr_in")
         scr_out = const.tile([P, 1], F32, name="scr_out")
         b1rows = const.tile([P, P], BF16, name="b1rows")
@@ -40,19 +44,20 @@ def tile_fp8modelwrapper_kernel(tc, x, w1_fp8, b1, w2_fp8, b2, out):
         nc.scalar.activation(out=scr_out[:], in_=scr_in[:], func=ACT.Gelu_apprx_tanh)
         ident = const.tile([P, P], F32, name="ident")
         make_identity(nc, ident[:])
+        ident_bf = const.tile([P, P], BF16, name="ident_bf")
+        nc.vector.tensor_copy(out=ident_bf[:], in_=ident[:])
 
         w1v = w1_fp8.rearrange("(g u q e) f -> g u q e f", g=2, u=2, q=P, e=2)
         w2v = w2_fp8.rearrange("(c s p) n -> c p s n", c=4, s=8, p=P)
         source = {}
 
         def load_w1_small(j):
+            t = const.tile([P, 8, 512], BF16, name="rs%d" % j)
             for g in range(2):
-                t = const.tile([P, 4, 512], BF16, name="rs%d_%d" % (j, g))
                 for u in range(2):
-                    nc.sync.dma_start(
-                        out=t[:, 2 * u : 2 * u + 2, :], in_=w1v[g, u][:, :, 512 * j : 512 * j + 512]
-                    )
-                source[(j, g)] = t[:]
+                    s = 4 * g + 2 * u
+                    nc.sync.dma_start(out=t[:, s : s + 2, :], in_=w1v[g, u][:, :, 512 * j : 512 * j + 512])
+            source[j] = t[:]
 
         def load_w1_chunk(i):
             t = rawp.tile([P, 8, 1024], BF16, name="raw1_%d" % i, tag="raw")
@@ -62,15 +67,15 @@ def tile_fp8modelwrapper_kernel(tc, x, w1_fp8, b1, w2_fp8, b2, out):
                     nc.sync.dma_start(
                         out=t[:, s : s + 2, :], in_=w1v[g, u][:, :, 1024 * i : 1024 * i + 1024]
                     )
-                for hf in range(2):
-                    source[(2 * i + hf, g)] = t[:, 4 * g : 4 * g + 4, 512 * hf : 512 * hf + 512]
+            for hf in range(2):
+                source[2 * i + hf] = t[:, :, 512 * hf : 512 * hf + 512]
 
         def load_w2_chunk(c):
             t = rawp.tile([P, 8, 1024], BF16, name="raw2_%d" % c, tag="raw")
             for g in range(2):
                 nc.sync.dma_start(out=t[:, 4 * g : 4 * g + 4, :], in_=w2v[c][:, 4 * g : 4 * g + 4, :])
-                for half in range(2):
-                    source[(8 + 4 * half + c, g)] = t[:, 4 * g : 4 * g + 4, 512 * half : 512 * half + 512]
+            for half in range(2):
+                source[8 + 4 * half + c] = t[:, :, 512 * half : 512 * half + 512]
 
         x_sb = const.tile([P, 4096], BF16, name="x_sb")
         x_sb3 = x_sb[:].rearrange("p (a k) -> p a k", a=4)
@@ -88,22 +93,45 @@ def tile_fp8modelwrapper_kernel(tc, x, w1_fp8, b1, w2_fp8, b2, out):
         grp = {}
         wcode = {}
         wscale = {}
+        zbank = {}
 
-        def regroup(copy, dst, src):
-            copy(
-                out=dst.rearrange("p (c i) t -> p c t i", i=4),
-                in_=src.rearrange("p t (c i) -> p c t i", i=4),
+        def fill_by_tensor(j):
+            for g in range(2):
+                z = bank("z%d_%d" % (j, g), 6 + g)
+                zbank[(j, g)] = z
+                words = z[:].rearrange("p (c u) -> p c u", u=2)
+                halves = z[:].bitcast(BF16).rearrange("p (c t) -> p c t", t=4)
+                for t in (1, 3, 0, 2):
+                    nc.tensor.matmul(
+                        out=words[:, :, t // 2] if t % 2 == 1 else halves[:, :, t],
+                        lhsT=ident_bf[:],
+                        rhs=source[j][:, 4 * g + t, 0:256],
+                        start=True,
+                        stop=True,
+                    )
+
+        def regroup_scalar(j):
+            grp[j] = grpp.tile([P, 2, 512, 4], BF16, name="grp%d" % j, tag="grp", align_bytes=64)
+            lo = TENSOR_COLUMNS[j]
+            hi = SCALAR_END[j]
+            if lo > 0:
+                for g in range(2):
+                    nc.scalar.copy(
+                        out=grp[j][:, g, 0:lo, :].rearrange("p c t -> p (c t)"),
+                        in_=zbank[(j, g)][:].bitcast(BF16),
+                    )
+            for g in range(2):
+                nc.scalar.copy(
+                    out=grp[j][:, g, lo:hi, :].rearrange("p (c i) t -> p c t i", i=4),
+                    in_=source[j][:, 4 * g : 4 * g + 4, lo:hi].rearrange("p t (c i) -> p c t i", i=4),
+                )
+
+        def regroup_vector(j):
+            lo = SCALAR_END[j]
+            nc.vector.tensor_copy(
+                out=grp[j][:, :, lo:512, :].rearrange("p g (c i) t -> p g c t i", i=4),
+                in_=source[j][:, :, lo:512].rearrange("p (g t) (c i) -> p g c t i", g=2, i=4),
             )
-
-        def regroup_scalar(j, g):
-            if g == 0:
-                grp[j] = grpp.tile([P, 2, 512, 4], BF16, name="grp%d" % j, tag="grp", align_bytes=64)
-            cs = SCALAR_COLUMNS[j]
-            regroup(nc.scalar.copy, grp[j][:, g, 0:cs, :], source[(j, g)][:, :, 0:cs])
-
-        def regroup_vector(j, g):
-            cs = SCALAR_COLUMNS[j]
-            regroup(nc.vector.tensor_copy, grp[j][:, g, cs:512, :], source[(j, g)][:, :, cs:512])
 
         def quantise_unit(j, parts):
             if 0 in parts:
@@ -123,7 +151,7 @@ def tile_fp8modelwrapper_kernel(tc, x, w1_fp8, b1, w2_fp8, b2, out):
         xt = {}
         for h in range(2):
             for g in range(2):
-                xt[(g, h)] = psum.tile([P, 512], F32, name="xt%d%d" % (g, h), tag="A%d" % (2 * h + g))
+                xt[(g, h)] = bank("xt%d%d" % (g, h), 2 * h + g)
                 for u in range(2):
                     for a2 in range(2):
                         a = 2 * h + a2
@@ -135,7 +163,7 @@ def tile_fp8modelwrapper_kernel(tc, x, w1_fp8, b1, w2_fp8, b2, out):
                         )
         b1f = const.tile([P, P], F32, name="b1f")
         nc.gpsimd.tensor_copy(out=b1f[:], in_=b1rows[:])
-        b1ps = psum.tile([P, 512], F32, name="b1ps", tag="B0")
+        b1ps = bank("b1ps", 4)
         nc.tensor.transpose(b1ps[:, 0:P], b1f[:], ident[:])
         b1col = const.tile([P, 32], F32, name="b1col")
 
@@ -150,11 +178,9 @@ def tile_fp8modelwrapper_kernel(tc, x, w1_fp8, b1, w2_fp8, b2, out):
         xscale = const.tile([P, 1024], U8, name="xscale", align_bytes=64)
         nc.vector.quantize_mx(out=xcode[:].bitcast(FP8X4), scales=xscale[:], in_=xg[:])
         nc.vector.tensor_copy(out=b1col[:], in_=b1ps[:, 0:32])
-        for g in range(2):
-            regroup_scalar(0, g)
-            regroup_vector(0, g)
-        for g in range(2):
-            regroup_scalar(1, g)
+        regroup_scalar(0)
+        regroup_vector(0)
+        regroup_scalar(1)
 
         hplane = {}
         hgrp = {}
@@ -162,11 +188,12 @@ def tile_fp8modelwrapper_kernel(tc, x, w1_fp8, b1, w2_fp8, b2, out):
         hscale = {}
         pm = {}
         acc = {}
+        acc_banks = {0: (2, 3, 6, 7), 1: (4, 5, 0, 1)}
         b2bc = const.tile([P, 1024], BF16, name="b2bc")
 
         def first_matmul(j):
             for m in range(4):
-                pm[(j, m)] = psum.tile([P, 512], F32, name="pm%d_%d" % (j, m), tag="%s%d" % ("AB"[j % 2], m))
+                pm[(j, m)] = bank("pm%d_%d" % (j, m), (4 * j + m) % 6)
                 for g in range(2):
                     cols = slice(512 * g + 128 * m, 512 * g + 128 * m + 128)
                     nc.tensor.matmul_mx(
@@ -192,7 +219,10 @@ def tile_fp8modelwrapper_kernel(tc, x, w1_fp8, b1, w2_fp8, b2, out):
 
         def regroup_h(j):
             hgrp[j] = hpool.tile([P, 512, 4], BF16, name="hg%d" % j, tag="hg", align_bytes=64)
-            regroup(nc.vector.tensor_copy, hgrp[j][:], hplane[j][:])
+            nc.vector.tensor_copy(
+                out=hgrp[j][:].rearrange("p (c i) t -> p c t i", i=4),
+                in_=hplane[j][:].rearrange("p t (c i) -> p c t i", i=4),
+            )
 
         def quantise_h(j):
             hcode[j] = const.tile([P, 512], U32, name="hc%d" % j, align_bytes=64)
@@ -209,9 +239,7 @@ def tile_fp8modelwrapper_kernel(tc, x, w1_fp8, b1, w2_fp8, b2, out):
             g = 2 * c + gi
             for a in range(4):
                 if g == 0:
-                    acc[(half, a)] = psum.tile(
-                        [P, 512], F32, name="acc%d_%d" % (half, a), tag="%s%d" % ("AB"[half], a)
-                    )
+                    acc[(half, a)] = bank("acc%d_%d" % (half, a), acc_banks[half][a])
                 nc.tensor.matmul_mx(
                     out=acc[(half, a)][:],
                     lhsT=hcode[g][:, 128 * a : 128 * a + 128].bitcast(FP8X4),
@@ -233,6 +261,10 @@ def tile_fp8modelwrapper_kernel(tc, x, w1_fp8, b1, w2_fp8, b2, out):
                 )
 
         for j in range(N_UNITS):
+            if 0 <= j - 1 < 8:
+                gelu(j - 1)
+            if j + 2 < N_UNITS and TENSOR_COLUMNS[j + 2] > 0:
+                fill_by_tensor(j + 2)
             if j == N_UNITS - 1:
                 for gi in range(2):
                     quantise_unit(j, (gi,))
@@ -246,17 +278,12 @@ def tile_fp8modelwrapper_kernel(tc, x, w1_fp8, b1, w2_fp8, b2, out):
                     second_matmul(j, 1)
             if j in FINISH_0:
                 finish(0, FINISH_0[j])
-            if j + 1 < N_UNITS:
-                regroup_vector(j + 1, 0)
             if 0 <= j - 2 < 8:
                 regroup_h(j - 2)
-            if 0 <= j - 1 < 8:
-                gelu(j - 1)
             if j + 2 < N_UNITS:
-                regroup_scalar(j + 2, 0)
-                regroup_scalar(j + 2, 1)
+                regroup_scalar(j + 2)
             if j + 1 < N_UNITS:
-                regroup_vector(j + 1, 1)
+                regroup_vector(j + 1)
             if 0 <= j - 2 < 8:
                 quantise_h(j - 2)
             if j == 4:

@@ -115,11 +115,9 @@ def tile_fp8modelwrapper_kernel(tc, x, w1_fp8, b1, w2_fp8, b2, out):
             lo = TENSOR_COLUMNS[j]
             hi = SCALAR_END[j]
             if lo > 0:
+                words = grp[j][:].rearrange("p g c t -> p (g c t)").bitcast(F32)
                 for g in range(2):
-                    nc.scalar.copy(
-                        out=grp[j][:, g, 0:lo, :].rearrange("p c t -> p (c t)"),
-                        in_=zbank[(j, g)][:].bitcast(BF16),
-                    )
+                    nc.scalar.copy(out=words[:, 1024 * g : 1024 * g + 2 * lo], in_=zbank[(j, g)][:])
             for g in range(2):
                 nc.scalar.copy(
                     out=grp[j][:, g, lo:hi, :].rearrange("p (c i) t -> p c t i", i=4),

@@ -15,8 +15,8 @@ ALU = mybir.AluOpType
 
 P = 128
 N_UNITS = 16
-TENSOR_COLUMNS = [0] * 3 + [256] * 7 + [0] * 6
-SCALAR_END = [320] * 2 + [216] + [304] * 7 + [264] * 4 + [456] * 2
+TENSOR_COLUMNS = [0] * 16
+SCALAR_END = [320] * 2 + [216] * 8 + [264] * 4 + [456] * 2
 FINISH_0 = {13: (0, 1), 14: (2, 3)}
 
 
@@ -30,7 +30,6 @@ def tile_fp8modelwrapper_kernel(tc, x, w1_fp8, b1, w2_fp8, b2, out):
         hpool = ctx.enter_context(tc.tile_pool(name="hpool", bufs=2))
         outp = ctx.enter_context(tc.tile_pool(name="outp", bufs=4))
         psum = ctx.enter_context(tc.psum_pool(name="psum", bufs=1))
-        ctx.enter_context(tc.manual_schedule())
 
         def bank(name, k):
             return psum.tile([P, 512], F32, name=name, tag="T%d" % k)
@@ -186,12 +185,12 @@ def tile_fp8modelwrapper_kernel(tc, x, w1_fp8, b1, w2_fp8, b2, out):
         hscale = {}
         pm = {}
         acc = {}
-        acc_banks = {0: (2, 3, 6, 7), 1: (4, 5, 0, 1)}
+        acc_banks = {0: (0, 1, 2, 3), 1: (4, 5, 6, 7)}
         b2bc = const.tile([P, 1024], BF16, name="b2bc")
 
         def first_matmul(j):
             for m in range(4):
-                pm[(j, m)] = bank("pm%d_%d" % (j, m), (4 * j + m) % 6)
+                pm[(j, m)] = bank("pm%d_%d" % (j, m), (4 * j + m) % 8)
                 for g in range(2):
                     cols = slice(512 * g + 128 * m, 512 * g + 128 * m + 128)
                     nc.tensor.matmul_mx(

@@ -15,8 +15,7 @@ ALU = mybir.AluOpType
 
 P = 128
 N_UNITS = 16
-TENSOR_COLUMNS = [0] * 16
-SCALAR_END = [320] * 2 + [216] * 8 + [264] * 4 + [456] * 2
+SCALAR_COLUMNS = [288] * 2 + [192] * 8 + [264] * 4 + [408] * 2
 FINISH_0 = {13: (0, 1), 14: (2, 3)}
 
 
@@ -30,9 +29,7 @@ def tile_fp8modelwrapper_kernel(tc, x, w1_fp8, b1, w2_fp8, b2, out):
         hpool = ctx.enter_context(tc.tile_pool(name="hpool", bufs=2))
         outp = ctx.enter_context(tc.tile_pool(name="outp", bufs=4))
         psum = ctx.enter_context(tc.psum_pool(name="psum", bufs=1))
-
-        def bank(name, k):
-            return psum.tile([P, 512], F32, name=name, tag="T%d" % k)
+        ctx.enter_context(tc.manual_schedule())
 
         scr_in = const.tile([P, 1], F32, name="scr_in")
         scr_out = const.tile([P, 1], F32, name="scr_out")
@@ -43,20 +40,19 @@ def tile_fp8modelwrapper_kernel(tc, x, w1_fp8, b1, w2_fp8, b2, out):
         nc.scalar.activation(out=scr_out[:], in_=scr_in[:], func=ACT.Gelu_apprx_tanh)
         ident = const.tile([P, P], F32, name="ident")
         make_identity(nc, ident[:])
-        ident_bf = const.tile([P, P], BF16, name="ident_bf")
-        nc.vector.tensor_copy(out=ident_bf[:], in_=ident[:])
 
         w1v = w1_fp8.rearrange("(g u q e) f -> g u q e f", g=2, u=2, q=P, e=2)
         w2v = w2_fp8.rearrange("(c s p) n -> c p s n", c=4, s=8, p=P)
         source = {}
 
         def load_w1_small(j):
-            t = const.tile([P, 8, 512], BF16, name="rs%d" % j)
             for g in range(2):
+                t = const.tile([P, 4, 512], BF16, name="rs%d_%d" % (j, g))
                 for u in range(2):
-                    s = 4 * g + 2 * u
-                    nc.sync.dma_start(out=t[:, s : s + 2, :], in_=w1v[g, u][:, :, 512 * j : 512 * j + 512])
-            source[j] = t[:]
+                    nc.sync.dma_start(
+                        out=t[:, 2 * u : 2 * u + 2, :], in_=w1v[g, u][:, :, 512 * j : 512 * j + 512]
+                    )
+                source[(j, g)] = t[:]
 
         def load_w1_chunk(i):
             t = rawp.tile([P, 8, 1024], BF16, name="raw1_%d" % i, tag="raw")
@@ -66,15 +62,15 @@ def tile_fp8modelwrapper_kernel(tc, x, w1_fp8, b1, w2_fp8, b2, out):
                     nc.sync.dma_start(
                         out=t[:, s : s + 2, :], in_=w1v[g, u][:, :, 1024 * i : 1024 * i + 1024]
                     )
-            for hf in range(2):
-                source[2 * i + hf] = t[:, :, 512 * hf : 512 * hf + 512]
+                for hf in range(2):
+                    source[(2 * i + hf, g)] = t[:, 4 * g : 4 * g + 4, 512 * hf : 512 * hf + 512]
 
         def load_w2_chunk(c):
             t = rawp.tile([P, 8, 1024], BF16, name="raw2_%d" % c, tag="raw")
             for g in range(2):
                 nc.sync.dma_start(out=t[:, 4 * g : 4 * g + 4, :], in_=w2v[c][:, 4 * g : 4 * g + 4, :])
-            for half in range(2):
-                source[8 + 4 * half + c] = t[:, :, 512 * half : 512 * half + 512]
+                for half in range(2):
+                    source[(8 + 4 * half + c, g)] = t[:, 4 * g : 4 * g + 4, 512 * half : 512 * half + 512]
 
         x_sb = const.tile([P, 4096], BF16, name="x_sb")
         x_sb3 = x_sb[:].rearrange("p (a k) -> p a k", a=4)
@@ -92,43 +88,22 @@ def tile_fp8modelwrapper_kernel(tc, x, w1_fp8, b1, w2_fp8, b2, out):
         grp = {}
         wcode = {}
         wscale = {}
-        zbank = {}
 
-        def fill_by_tensor(j):
-            for g in range(2):
-                z = bank("z%d_%d" % (j, g), 6 + g)
-                zbank[(j, g)] = z
-                words = z[:].rearrange("p (c u) -> p c u", u=2)
-                halves = z[:].bitcast(BF16).rearrange("p (c t) -> p c t", t=4)
-                for t in (1, 3, 0, 2):
-                    nc.tensor.matmul(
-                        out=words[:, :, t // 2] if t % 2 == 1 else halves[:, :, t],
-                        lhsT=ident_bf[:],
-                        rhs=source[j][:, 4 * g + t, 0:256],
-                        start=True,
-                        stop=True,
-                    )
-
-        def regroup_scalar(j):
-            grp[j] = grpp.tile([P, 2, 512, 4], BF16, name="grp%d" % j, tag="grp", align_bytes=64)
-            lo = TENSOR_COLUMNS[j]
-            hi = SCALAR_END[j]
-            if lo > 0:
-                words = grp[j][:].rearrange("p g c t -> p (g c t)").bitcast(F32)
-                for g in range(2):
-                    nc.scalar.copy(out=words[:, 1024 * g : 1024 * g + 2 * lo], in_=zbank[(j, g)][:])
-            for g in range(2):
-                nc.scalar.copy(
-                    out=grp[j][:, g, lo:hi, :].rearrange("p (c i) t -> p c t i", i=4),
-                    in_=source[j][:, 4 * g : 4 * g + 4, lo:hi].rearrange("p t (c i) -> p c t i", i=4),
-                )
-
-        def regroup_vector(j):
-            lo = SCALAR_END[j]
-            nc.vector.tensor_copy(
-                out=grp[j][:, :, lo:512, :].rearrange("p g (c i) t -> p g c t i", i=4),
-                in_=source[j][:, :, lo:512].rearrange("p (g t) (c i) -> p g c t i", g=2, i=4),
+        def regroup(copy, dst, src):
+            copy(
+                out=dst.rearrange("p (c i) t -> p c t i", i=4),
+                in_=src.rearrange("p t (c i) -> p c t i", i=4),
             )
+
+        def regroup_scalar(j, g):
+            if g == 0:
+                grp[j] = grpp.tile([P, 2, 512, 4], BF16, name="grp%d" % j, tag="grp", align_bytes=64)
+            cs = SCALAR_COLUMNS[j]
+            regroup(nc.scalar.copy, grp[j][:, g, 0:cs, :], source[(j, g)][:, :, 0:cs])
+
+        def regroup_vector(j, g):
+            cs = SCALAR_COLUMNS[j]
+            regroup(nc.vector.tensor_copy, grp[j][:, g, cs:512, :], source[(j, g)][:, :, cs:512])
 
         def quantise_unit(j, parts):
             if 0 in parts:
@@ -148,7 +123,7 @@ def tile_fp8modelwrapper_kernel(tc, x, w1_fp8, b1, w2_fp8, b2, out):
         xt = {}
         for h in range(2):
             for g in range(2):
-                xt[(g, h)] = bank("xt%d%d" % (g, h), 2 * h + g)
+                xt[(g, h)] = psum.tile([P, 512], F32, name="xt%d%d" % (g, h), tag="A%d" % (2 * h + g))
                 for u in range(2):
                     for a2 in range(2):
                         a = 2 * h + a2
@@ -160,7 +135,7 @@ def tile_fp8modelwrapper_kernel(tc, x, w1_fp8, b1, w2_fp8, b2, out):
                         )
         b1f = const.tile([P, P], F32, name="b1f")
         nc.gpsimd.tensor_copy(out=b1f[:], in_=b1rows[:])
-        b1ps = bank("b1ps", 4)
+        b1ps = psum.tile([P, 512], F32, name="b1ps", tag="B0")
         nc.tensor.transpose(b1ps[:, 0:P], b1f[:], ident[:])
         b1col = const.tile([P, 32], F32, name="b1col")
 
@@ -175,9 +150,11 @@ def tile_fp8modelwrapper_kernel(tc, x, w1_fp8, b1, w2_fp8, b2, out):
         xscale = const.tile([P, 1024], U8, name="xscale", align_bytes=64)
         nc.vector.quantize_mx(out=xcode[:].bitcast(FP8X4), scales=xscale[:], in_=xg[:])
         nc.vector.tensor_copy(out=b1col[:], in_=b1ps[:, 0:32])
-        regroup_scalar(0)
-        regroup_vector(0)
-        regroup_scalar(1)
+        for g in range(2):
+            regroup_scalar(0, g)
+            regroup_vector(0, g)
+        for g in range(2):
+            regroup_scalar(1, g)
 
         hplane = {}
         hgrp = {}
@@ -185,12 +162,11 @@ def tile_fp8modelwrapper_kernel(tc, x, w1_fp8, b1, w2_fp8, b2, out):
         hscale = {}
         pm = {}
         acc = {}
-        acc_banks = {0: (0, 1, 2, 3), 1: (4, 5, 6, 7)}
         b2bc = const.tile([P, 1024], BF16, name="b2bc")
 
         def first_matmul(j):
             for m in range(4):
-                pm[(j, m)] = bank("pm%d_%d" % (j, m), (4 * j + m) % 8)
+                pm[(j, m)] = psum.tile([P, 512], F32, name="pm%d_%d" % (j, m), tag="%s%d" % ("AB"[j % 2], m))
                 for g in range(2):
                     cols = slice(512 * g + 128 * m, 512 * g + 128 * m + 128)
                     nc.tensor.matmul_mx(
@@ -216,10 +192,7 @@ def tile_fp8modelwrapper_kernel(tc, x, w1_fp8, b1, w2_fp8, b2, out):
 
         def regroup_h(j):
             hgrp[j] = hpool.tile([P, 512, 4], BF16, name="hg%d" % j, tag="hg", align_bytes=64)
-            nc.vector.tensor_copy(
-                out=hgrp[j][:].rearrange("p (c i) t -> p c t i", i=4),
-                in_=hplane[j][:].rearrange("p t (c i) -> p c t i", i=4),
-            )
+            regroup(nc.vector.tensor_copy, hgrp[j][:], hplane[j][:])
 
         def quantise_h(j):
             hcode[j] = const.tile([P, 512], U32, name="hc%d" % j, align_bytes=64)
@@ -236,7 +209,9 @@ def tile_fp8modelwrapper_kernel(tc, x, w1_fp8, b1, w2_fp8, b2, out):
             g = 2 * c + gi
             for a in range(4):
                 if g == 0:
-                    acc[(half, a)] = bank("acc%d_%d" % (half, a), acc_banks[half][a])
+                    acc[(half, a)] = psum.tile(
+                        [P, 512], F32, name="acc%d_%d" % (half, a), tag="%s%d" % ("AB"[half], a)
+                    )
                 nc.tensor.matmul_mx(
                     out=acc[(half, a)][:],
                     lhsT=hcode[g][:, 128 * a : 128 * a + 128].bitcast(FP8X4),
@@ -258,10 +233,6 @@ def tile_fp8modelwrapper_kernel(tc, x, w1_fp8, b1, w2_fp8, b2, out):
                 )
 
         for j in range(N_UNITS):
-            if 0 <= j - 1 < 8:
-                gelu(j - 1)
-            if j + 2 < N_UNITS and TENSOR_COLUMNS[j + 2] > 0:
-                fill_by_tensor(j + 2)
             if j == N_UNITS - 1:
                 for gi in range(2):
                     quantise_unit(j, (gi,))
@@ -275,12 +246,17 @@ def tile_fp8modelwrapper_kernel(tc, x, w1_fp8, b1, w2_fp8, b2, out):
                     second_matmul(j, 1)
             if j in FINISH_0:
                 finish(0, FINISH_0[j])
+            if j + 1 < N_UNITS:
+                regroup_vector(j + 1, 0)
             if 0 <= j - 2 < 8:
                 regroup_h(j - 2)
+            if 0 <= j - 1 < 8:
+                gelu(j - 1)
             if j + 2 < N_UNITS:
-                regroup_scalar(j + 2)
+                regroup_scalar(j + 2, 0)
+                regroup_scalar(j + 2, 1)
             if j + 1 < N_UNITS:
-                regroup_vector(j + 1)
+                regroup_vector(j + 1, 1)
             if 0 <= j - 2 < 8:
                 quantise_h(j - 2)
             if j == 4:

@@ -15,7 +15,11 @@ ALU = mybir.AluOpType
 
 P = 128
 N_UNITS = 16
-SCALAR_COLUMNS = [288] * 2 + [192] * 8 + [264] * 4 + [408] * 2
+TENSOR = [0] * 3 + [256] * 7 + [0] * 6
+SCALAR_END = (
+    [288] * 2 + [216] + [256] * 7 + [264] * 4 + [408] * 2,
+    [288] * 2 + [216] + [264] * 7 + [264] * 4 + [408] * 2,
+)
 FINISH_0 = {13: (0, 1), 14: (2, 3)}
 
 
@@ -31,6 +35,9 @@ def tile_fp8modelwrapper_kernel(tc, x, w1_fp8, b1, w2_fp8, b2, out):
         psum = ctx.enter_context(tc.psum_pool(name="psum", bufs=1))
         ctx.enter_context(tc.manual_schedule())
 
+        def bank(name, k):
+            return psum.tile([P, 512], F32, name=name, tag="T%d" % k)
+
         scr_in = const.tile([P, 1], F32, name="scr_in")
         scr_out = const.tile([P, 1], F32, name="scr_out")
         b1rows = const.tile([P, P], BF16, name="b1rows")
@@ -40,6 +47,8 @@ def tile_fp8modelwrapper_kernel(tc, x, w1_fp8, b1, w2_fp8, b2, out):
         nc.scalar.activation(out=scr_out[:], in_=scr_in[:], func=ACT.Gelu_apprx_tanh)
         ident = const.tile([P, P], F32, name="ident")
         make_identity(nc, ident[:])
+        ident_bf = const.tile([P, P], BF16, name="ident_bf")
+        nc.vector.tensor_copy(out=ident_bf[:], in_=ident[:])
 
         w1v = w1_fp8.rearrange("(g u q e) f -> g u q e f", g=2, u=2, q=P, e=2)
         w2v = w2_fp8.rearrange("(c s p) n -> c p s n", c=4, s=8, p=P)
@@ -95,15 +104,36 @@ def tile_fp8modelwrapper_kernel(tc, x, w1_fp8, b1, w2_fp8, b2, out):
                 in_=src.rearrange("p t (c i) -> p c t i", i=4),
             )
 
+        zbank = {}
+
+        def fill_by_tensor(j):
+            z = bank("z%d" % j, 7)
+            zbank[j] = z
+            words = z[:].rearrange("p (c u) -> p c u", u=2)
+            halves = z[:].bitcast(BF16).rearrange("p (c t) -> p c t", t=4)
+            for t in (1, 3, 0, 2):
+                nc.tensor.matmul(
+                    out=words[:, :, t // 2] if t % 2 == 1 else halves[:, :, t],
+                    lhsT=ident_bf[:],
+                    rhs=source[(j, 0)][:, t, 0:256],
+                    start=True,
+                    stop=True,
+                )
+
         def regroup_scalar(j, g):
             if g == 0:
                 grp[j] = grpp.tile([P, 2, 512, 4], BF16, name="grp%d" % j, tag="grp", align_bytes=64)
-            cs = SCALAR_COLUMNS[j]
-            regroup(nc.scalar.copy, grp[j][:, g, 0:cs, :], source[(j, g)][:, :, 0:cs])
+            lo = TENSOR[j] if g == 0 else 0
+            hi = SCALAR_END[g][j]
+            if lo > 0:
+                words = grp[j][:].rearrange("p g c t -> p (g c t)").bitcast(F32)
+                nc.scalar.copy(out=words[:, 0 : 2 * lo], in_=zbank[j][:])
+            if hi > lo:
+                regroup(nc.scalar.copy, grp[j][:, g, lo:hi, :], source[(j, g)][:, :, lo:hi])
 
         def regroup_vector(j, g):
-            cs = SCALAR_COLUMNS[j]
-            regroup(nc.vector.tensor_copy, grp[j][:, g, cs:512, :], source[(j, g)][:, :, cs:512])
+            lo = SCALAR_END[g][j]
+            regroup(nc.vector.tensor_copy, grp[j][:, g, lo:512, :], source[(j, g)][:, :, lo:512])
 
         def quantise_unit(j, parts):
             if 0 in parts:
@@ -123,7 +153,7 @@ def tile_fp8modelwrapper_kernel(tc, x, w1_fp8, b1, w2_fp8, b2, out):
         xt = {}
         for h in range(2):
             for g in range(2):
-                xt[(g, h)] = psum.tile([P, 512], F32, name="xt%d%d" % (g, h), tag="A%d" % (2 * h + g))
+                xt[(g, h)] = bank("xt%d%d" % (g, h), 2 * h + g)
                 for u in range(2):
                     for a2 in range(2):
                         a = 2 * h + a2
@@ -135,7 +165,7 @@ def tile_fp8modelwrapper_kernel(tc, x, w1_fp8, b1, w2_fp8, b2, out):
                         )
         b1f = const.tile([P, P], F32, name="b1f")
         nc.gpsimd.tensor_copy(out=b1f[:], in_=b1rows[:])
-        b1ps = psum.tile([P, 512], F32, name="b1ps", tag="B0")
+        b1ps = bank("b1ps", 4)
         nc.tensor.transpose(b1ps[:, 0:P], b1f[:], ident[:])
         b1col = const.tile([P, 32], F32, name="b1col")
 
@@ -166,7 +196,7 @@ def tile_fp8modelwrapper_kernel(tc, x, w1_fp8, b1, w2_fp8, b2, out):
 
         def first_matmul(j):
             for m in range(4):
-                pm[(j, m)] = psum.tile([P, 512], F32, name="pm%d_%d" % (j, m), tag="%s%d" % ("AB"[j % 2], m))
+                pm[(j, m)] = bank("pm%d_%d" % (j, m), (4 * j + m) % 7)
                 for g in range(2):
                     cols = slice(512 * g + 128 * m, 512 * g + 128 * m + 128)
                     nc.tensor.matmul_mx(
@@ -209,9 +239,7 @@ def tile_fp8modelwrapper_kernel(tc, x, w1_fp8, b1, w2_fp8, b2, out):
             g = 2 * c + gi
             for a in range(4):
                 if g == 0:
-                    acc[(half, a)] = psum.tile(
-                        [P, 512], F32, name="acc%d_%d" % (half, a), tag="%s%d" % ("AB"[half], a)
-                    )
+                    acc[(half, a)] = bank("acc%d_%d" % (half, a), 4 - 4 * half + a)
                 nc.tensor.matmul_mx(
                     out=acc[(half, a)][:],
                     lhsT=hcode[g][:, 128 * a : 128 * a + 128].bitcast(FP8X4),
@@ -233,6 +261,10 @@ def tile_fp8modelwrapper_kernel(tc, x, w1_fp8, b1, w2_fp8, b2, out):
                 )
 
         for j in range(N_UNITS):
+            if 0 <= j - 1 < 8:
+                gelu(j - 1)
+            if j + 2 < N_UNITS and TENSOR[j + 2] > 0:
+                fill_by_tensor(j + 2)
             if j == N_UNITS - 1:
                 for gi in range(2):
                     quantise_unit(j, (gi,))
@@ -250,8 +282,6 @@ def tile_fp8modelwrapper_kernel(tc, x, w1_fp8, b1, w2_fp8, b2, out):
                 regroup_vector(j + 1, 0)
             if 0 <= j - 2 < 8:
                 regroup_h(j - 2)
-            if 0 <= j - 1 < 8:
-                gelu(j - 1)
             if j + 2 < N_UNITS:
                 regroup_scalar(j + 2, 0)
                 regroup_scalar(j + 2, 1)

@@ -15,11 +15,8 @@ ALU = mybir.AluOpType
 
 P = 128
 N_UNITS = 16
-TENSOR = [0] * 3 + [256] * 7 + [0] * 6
-SCALAR_END = (
-    [288] * 2 + [216] + [256] * 7 + [264] * 4 + [408] * 2,
-    [288] * 2 + [216] + [264] * 7 + [264] * 4 + [408] * 2,
-)
+TENSOR_COLUMNS = [0] * 16
+SCALAR_END = [320] * 2 + [216] * 8 + [264] * 4 + [456] * 2
 FINISH_0 = {13: (0, 1), 14: (2, 3)}
 
 
@@ -55,13 +52,12 @@ def tile_fp8modelwrapper_kernel(tc, x, w1_fp8, b1, w2_fp8, b2, out):
         source = {}
 
         def load_w1_small(j):
+            t = const.tile([P, 8, 512], BF16, name="rs%d" % j)
             for g in range(2):
-                t = const.tile([P, 4, 512], BF16, name="rs%d_%d" % (j, g))
                 for u in range(2):
-                    nc.sync.dma_start(
-                        out=t[:, 2 * u : 2 * u + 2, :], in_=w1v[g, u][:, :, 512 * j : 512 * j + 512]
-                    )
-                source[(j, g)] = t[:]
+                    s = 4 * g + 2 * u
+                    nc.sync.dma_start(out=t[:, s : s + 2, :], in_=w1v[g, u][:, :, 512 * j : 512 * j + 512])
+            source[j] = t[:]
 
         def load_w1_chunk(i):
             t = rawp.tile([P, 8, 1024], BF16, name="raw1_%d" % i, tag="raw")
@@ -71,15 +67,15 @@ def tile_fp8modelwrapper_kernel(tc, x, w1_fp8, b1, w2_fp8, b2, out):
                     nc.sync.dma_start(
                         out=t[:, s : s + 2, :], in_=w1v[g, u][:, :, 1024 * i : 1024 * i + 1024]
                     )
-                for hf in range(2):
-                    source[(2 * i + hf, g)] = t[:, 4 * g : 4 * g + 4, 512 * hf : 512 * hf + 512]
+            for hf in range(2):
+                source[2 * i + hf] = t[:, :, 512 * hf : 512 * hf + 512]
 
         def load_w2_chunk(c):
             t = rawp.tile([P, 8, 1024], BF16, name="raw2_%d" % c, tag="raw")
             for g in range(2):
                 nc.sync.dma_start(out=t[:, 4 * g : 4 * g + 4, :], in_=w2v[c][:, 4 * g : 4 * g + 4, :])
-                for half in range(2):
-                    source[(8 + 4 * half + c, g)] = t[:, 4 * g : 4 * g + 4, 512 * half : 512 * half + 512]
+            for half in range(2):
+                source[8 + 4 * half + c] = t[:, :, 512 * half : 512 * half + 512]
 
         x_sb = const.tile([P, 4096], BF16, name="x_sb")
         x_sb3 = x_sb[:].rearrange("p (a k) -> p a k", a=4)
@@ -97,43 +93,43 @@ def tile_fp8modelwrapper_kernel(tc, x, w1_fp8, b1, w2_fp8, b2, out):
         grp = {}
         wcode = {}
         wscale = {}
-
-        def regroup(copy, dst, src):
-            copy(
-                out=dst.rearrange("p (c i) t -> p c t i", i=4),
-                in_=src.rearrange("p t (c i) -> p c t i", i=4),
-            )
-
         zbank = {}
 
         def fill_by_tensor(j):
-            z = bank("z%d" % j, 7)
-            zbank[j] = z
-            words = z[:].rearrange("p (c u) -> p c u", u=2)
-            halves = z[:].bitcast(BF16).rearrange("p (c t) -> p c t", t=4)
-            for t in (1, 3, 0, 2):
-                nc.tensor.matmul(
-                    out=words[:, :, t // 2] if t % 2 == 1 else halves[:, :, t],
-                    lhsT=ident_bf[:],
-                    rhs=source[(j, 0)][:, t, 0:256],
-                    start=True,
-                    stop=True,
-                )
+            for g in range(2):
+                z = bank("z%d_%d" % (j, g), 6 + g)
+                zbank[(j, g)] = z
+                words = z[:].rearrange("p (c u) -> p c u", u=2)
+                halves = z[:].bitcast(BF16).rearrange("p (c t) -> p c t", t=4)
+                for t in (1, 3, 0, 2):
+                    nc.tensor.matmul(
+                        out=words[:, :, t // 2] if t % 2 == 1 else halves[:, :, t],
+                        lhsT=ident_bf[:],
+                        rhs=source[j][:, 4 * g + t, 0:256],
+                        start=True,
+                        stop=True,
+                    )
 
-        def regroup_scalar(j, g):
-            if g == 0:
-                grp[j] = grpp.tile([P, 2, 512, 4], BF16, name="grp%d" % j, tag="grp", align_bytes=64)
-            lo = TENSOR[j] if g == 0 else 0
-            hi = SCALAR_END[g][j]
+        def regroup_scalar(j):
+            grp[j] = grpp.tile([P, 2, 512, 4], BF16, name="grp%d" % j, tag="grp", align_bytes=64)
+            lo = TENSOR_COLUMNS[j]
+            hi = SCALAR_END[j]
             if lo > 0:
                 words = grp[j][:].rearrange("p g c t -> p (g c t)").bitcast(F32)
-                nc.scalar.copy(out=words[:, 0 : 2 * lo], in_=zbank[j][:])
-            if hi > lo:
-                regroup(nc.scalar.copy, grp[j][:, g, lo:hi, :], source[(j, g)][:, :, lo:hi])
+                for g in range(2):
+                    nc.scalar.copy(out=words[:, 1024 * g : 1024 * g + 2 * lo], in_=zbank[(j, g)][:])
+            for g in range(2):
+                nc.scalar.copy(
+                    out=grp[j][:, g, lo:hi, :].rearrange("p (c i) t -> p c t i", i=4),
+                    in_=source[j][:, 4 * g : 4 * g + 4, lo:hi].rearrange("p t (c i) -> p c t i", i=4),
+                )
 
-        def regroup_vector(j, g):
-            lo = SCALAR_END[g][j]
-            regroup(nc.vector.tensor_copy, grp[j][:, g, lo:512, :], source[(j, g)][:, :, lo:512])
+        def regroup_vector(j):
+            lo = SCALAR_END[j]
+            nc.vector.tensor_copy(
+                out=grp[j][:, :, lo:512, :].rearrange("p g (c i) t -> p g c t i", i=4),
+                in_=source[j][:, :, lo:512].rearrange("p (g t) (c i) -> p g c t i", g=2, i=4),
+            )
 
         def quantise_unit(j, parts):
             if 0 in parts:
@@ -180,11 +176,9 @@ def tile_fp8modelwrapper_kernel(tc, x, w1_fp8, b1, w2_fp8, b2, out):
         xscale = const.tile([P, 1024], U8, name="xscale", align_bytes=64)
         nc.vector.quantize_mx(out=xcode[:].bitcast(FP8X4), scales=xscale[:], in_=xg[:])
         nc.vector.tensor_copy(out=b1col[:], in_=b1ps[:, 0:32])
-        for g in range(2):
-            regroup_scalar(0, g)
-            regroup_vector(0, g)
-        for g in range(2):
-            regroup_scalar(1, g)
+        regroup_scalar(0)
+        regroup_vector(0)
+        regroup_scalar(1)
 
         hplane = {}
         hgrp = {}
@@ -192,11 +186,12 @@ def tile_fp8modelwrapper_kernel(tc, x, w1_fp8, b1, w2_fp8, b2, out):
         hscale = {}
         pm = {}
         acc = {}
+        acc_banks = {0: (0, 1, 2, 3), 1: (4, 5, 6, 7)}
         b2bc = const.tile([P, 1024], BF16, name="b2bc")
 
         def first_matmul(j):
             for m in range(4):
-                pm[(j, m)] = bank("pm%d_%d" % (j, m), (4 * j + m) % 7)
+                pm[(j, m)] = bank("pm%d_%d" % (j, m), (4 * j + m) % 8)
                 for g in range(2):
                     cols = slice(512 * g + 128 * m, 512 * g + 128 * m + 128)
                     nc.tensor.matmul_mx(
@@ -222,7 +217,10 @@ def tile_fp8modelwrapper_kernel(tc, x, w1_fp8, b1, w2_fp8, b2, out):
 
         def regroup_h(j):
             hgrp[j] = hpool.tile([P, 512, 4], BF16, name="hg%d" % j, tag="hg", align_bytes=64)
-            regroup(nc.vector.tensor_copy, hgrp[j][:], hplane[j][:])
+            nc.vector.tensor_copy(
+                out=hgrp[j][:].rearrange("p (c i) t -> p c t i", i=4),
+                in_=hplane[j][:].rearrange("p t (c i) -> p c t i", i=4),
+            )
 
         def quantise_h(j):
             hcode[j] = const.tile([P, 512], U32, name="hc%d" % j, align_bytes=64)
@@ -239,7 +237,7 @@ def tile_fp8modelwrapper_kernel(tc, x, w1_fp8, b1, w2_fp8, b2, out):
             g = 2 * c + gi
             for a in range(4):
                 if g == 0:
-                    acc[(half, a)] = bank("acc%d_%d" % (half, a), 4 - 4 * half + a)
+                    acc[(half, a)] = bank("acc%d_%d" % (half, a), acc_banks[half][a])
                 nc.tensor.matmul_mx(
                     out=acc[(half, a)][:],
                     lhsT=hcode[g][:, 128 * a : 128 * a + 128].bitcast(FP8X4),
@@ -263,7 +261,7 @@ def tile_fp8modelwrapper_kernel(tc, x, w1_fp8, b1, w2_fp8, b2, out):
         for j in range(N_UNITS):
             if 0 <= j - 1 < 8:
                 gelu(j - 1)
-            if j + 2 < N_UNITS and TENSOR[j + 2] > 0:
+            if j + 2 < N_UNITS and TENSOR_COLUMNS[j + 2] > 0:
                 fill_by_tensor(j + 2)
             if j == N_UNITS - 1:
                 for gi in range(2):
@@ -278,15 +276,12 @@ def tile_fp8modelwrapper_kernel(tc, x, w1_fp8, b1, w2_fp8, b2, out):
                     second_matmul(j, 1)
             if j in FINISH_0:
                 finish(0, FINISH_0[j])
-            if j + 1 < N_UNITS:
-                regroup_vector(j + 1, 0)
             if 0 <= j - 2 < 8:
                 regroup_h(j - 2)
             if j + 2 < N_UNITS:
-                regroup_scalar(j + 2, 0)
-                regroup_scalar(j + 2, 1)
+                regroup_scalar(j + 2)
             if j + 1 < N_UNITS:
-                regroup_vector(j + 1, 1)
+                regroup_vector(j + 1)
             if 0 <= j - 2 < 8:
                 quantise_h(j - 2)
             if j == 4:

from contextlib import ExitStack

import concourse.mybir as mybir
from concourse.masks import make_identity

FLOPS = 2 * 512 * 1024 * 4096 * 2

F32 = mybir.dt.float32
BF16 = mybir.dt.bfloat16
U32 = mybir.dt.uint32
U8 = mybir.dt.uint8
FP8X4 = mybir.dt.float8_e4m3fn_x4
ACT = mybir.ActivationFunctionType
ALU = mybir.AluOpType

P = 128
N_UNITS = 16
TENSOR_COLUMNS = [0] * 16
SCALAR_END = [320] * 2 + [216] * 8 + [264] * 4 + [456] * 2
FINISH_0 = {13: (0, 1), 14: (2, 3)}


def tile_fp8modelwrapper_kernel(tc, x, w1_fp8, b1, w2_fp8, b2, out):
    nc = tc.nc
    with ExitStack() as ctx:
        const = ctx.enter_context(tc.tile_pool(name="const", bufs=1))
        rawp = ctx.enter_context(tc.tile_pool(name="rawp", bufs=5))
        grpp = ctx.enter_context(tc.tile_pool(name="grpp", bufs=3))
        codep = ctx.enter_context(tc.tile_pool(name="codep", bufs=3))
        hpool = ctx.enter_context(tc.tile_pool(name="hpool", bufs=2))
        outp = ctx.enter_context(tc.tile_pool(name="outp", bufs=4))
        psum = ctx.enter_context(tc.psum_pool(name="psum", bufs=1))
        ctx.enter_context(tc.manual_schedule())

        def bank(name, k):
            return psum.tile([P, 512], F32, name=name, tag="T%d" % k)

        scr_in = const.tile([P, 1], F32, name="scr_in")
        scr_out = const.tile([P, 1], F32, name="scr_out")
        b1rows = const.tile([P, P], BF16, name="b1rows")
        nc.vector.memset(b1rows[:], 0.0)
        nc.vector.memset(scr_in[:], 0.0)
        nc.scalar.dma_start(out=b1rows[0:32, :], in_=b1.rearrange("(r c) -> r c", c=P))
        nc.scalar.activation(out=scr_out[:], in_=scr_in[:], func=ACT.Gelu_apprx_tanh)
        ident = const.tile([P, P], F32, name="ident")
        make_identity(nc, ident[:])
        ident_bf = const.tile([P, P], BF16, name="ident_bf")
        nc.vector.tensor_copy(out=ident_bf[:], in_=ident[:])

        w1v = w1_fp8.rearrange("(g u q e) f -> g u q e f", g=2, u=2, q=P, e=2)
        w2v = w2_fp8.rearrange("(c s p) n -> c p s n", c=4, s=8, p=P)
        source = {}

        def load_w1_small(j):
            t = const.tile([P, 8, 512], BF16, name="rs%d" % j)
            for g in range(2):
                for u in range(2):
                    s = 4 * g + 2 * u
                    nc.sync.dma_start(out=t[:, s : s + 2, :], in_=w1v[g, u][:, :, 512 * j : 512 * j + 512])
            source[j] = t[:]

        def load_w1_chunk(i):
            t = rawp.tile([P, 8, 1024], BF16, name="raw1_%d" % i, tag="raw")
            for g in range(2):
                for u in range(2):
                    s = 4 * g + 2 * u
                    nc.sync.dma_start(
                        out=t[:, s : s + 2, :], in_=w1v[g, u][:, :, 1024 * i : 1024 * i + 1024]
                    )
            for hf in range(2):
                source[2 * i + hf] = t[:, :, 512 * hf : 512 * hf + 512]

        def load_w2_chunk(c):
            t = rawp.tile([P, 8, 1024], BF16, name="raw2_%d" % c, tag="raw")
            for g in range(2):
                nc.sync.dma_start(out=t[:, 4 * g : 4 * g + 4, :], in_=w2v[c][:, 4 * g : 4 * g + 4, :])
            for half in range(2):
                source[8 + 4 * half + c] = t[:, :, 512 * half : 512 * half + 512]

        x_sb = const.tile([P, 4096], BF16, name="x_sb")
        x_sb3 = x_sb[:].rearrange("p (a k) -> p a k", a=4)
        xv = x.rearrange("(a p) k -> p a k", p=P)
        nc.sync.dma_start(out=x_sb3[:, 0:2, :], in_=xv[:, 0:2, :])
        nc.sync.dma_start(out=x_sb3[:, 2:4, :], in_=xv[:, 2:4, :])
        for j in range(4):
            load_w1_small(j)
        load_w1_chunk(2)
        load_w1_chunk(3)
        load_w2_chunk(0)
        load_w2_chunk(1)
        load_w2_chunk(2)

        grp = {}
        wcode = {}
        wscale = {}
        zbank = {}

        def fill_by_tensor(j):
            for g in range(2):
                z = bank("z%d_%d" % (j, g), 6 + g)
                zbank[(j, g)] = z
                words = z[:].rearrange("p (c u) -> p c u", u=2)
                halves = z[:].bitcast(BF16).rearrange("p (c t) -> p c t", t=4)
                for t in (1, 3, 0, 2):
                    nc.tensor.matmul(
                        out=words[:, :, t // 2] if t % 2 == 1 else halves[:, :, t],
                        lhsT=ident_bf[:],
                        rhs=source[j][:, 4 * g + t, 0:256],
                        start=True,
                        stop=True,
                    )

        def regroup_scalar(j):
            grp[j] = grpp.tile([P, 2, 512, 4], BF16, name="grp%d" % j, tag="grp", align_bytes=64)
            lo = TENSOR_COLUMNS[j]
            hi = SCALAR_END[j]
            if lo > 0:
                words = grp[j][:].rearrange("p g c t -> p (g c t)").bitcast(F32)
                for g in range(2):
                    nc.scalar.copy(out=words[:, 1024 * g : 1024 * g + 2 * lo], in_=zbank[(j, g)][:])
            for g in range(2):
                nc.scalar.copy(
                    out=grp[j][:, g, lo:hi, :].rearrange("p (c i) t -> p c t i", i=4),
                    in_=source[j][:, 4 * g : 4 * g + 4, lo:hi].rearrange("p t (c i) -> p c t i", i=4),
                )

        def regroup_vector(j):
            lo = SCALAR_END[j]
            nc.vector.tensor_copy(
                out=grp[j][:, :, lo:512, :].rearrange("p g (c i) t -> p g c t i", i=4),
                in_=source[j][:, :, lo:512].rearrange("p (g t) (c i) -> p g c t i", g=2, i=4),
            )

        def quantise_unit(j, parts):
            if 0 in parts:
                wcode[j] = codep.tile([P, 1024], U32, name="wc%d" % j, tag="wc", align_bytes=64)
                wscale[j] = codep.tile([P, 1024], U8, name="ws%d" % j, tag="ws", align_bytes=64)
            lo = 512 * parts[0]
            hi = 512 * parts[-1] + 512
            nc.vector.quantize_mx(
                out=wcode[j][:, lo:hi].bitcast(FP8X4),
                scales=wscale[j][:, lo:hi],
                in_=grp[j][:, parts[0] : parts[-1] + 1, :, :].rearrange("p g c t -> p (g c t)"),
            )

        xw = x_sb[:].bitcast(F32)
        xg = const.tile([P, 4096], BF16, name="xg", align_bytes=64)
        xgw = xg[:].bitcast(F32).rearrange("p (g w u) -> p g w u", g=2, u=2)
        xt = {}
        for h in range(2):
            for g in range(2):
                xt[(g, h)] = bank("xt%d%d" % (g, h), 2 * h + g)
                for u in range(2):
                    for a2 in range(2):
                        a = 2 * h + a2
                        col = 512 * a + 256 * g + 128 * u
                        nc.tensor.transpose(
                            xt[(g, h)][:, 256 * u + 128 * a2 : 256 * u + 128 * a2 + 128],
                            xw[:, col : col + 128],
                            ident[:],
                        )
        b1f = const.tile([P, P], F32, name="b1f")
        nc.gpsimd.tensor_copy(out=b1f[:], in_=b1rows[:])
        b1ps = bank("b1ps", 4)
        nc.tensor.transpose(b1ps[:, 0:P], b1f[:], ident[:])
        b1col = const.tile([P, 32], F32, name="b1col")

        for h in range(2):
            for g in range(2):
                copy = nc.scalar.copy if g == 0 else nc.vector.tensor_copy
                copy(
                    out=xgw[:, g, 256 * h : 256 * h + 256, :],
                    in_=xt[(g, h)][:].rearrange("p (u w) -> p w u", u=2),
                )
        xcode = const.tile([P, 1024], U32, name="xcode", align_bytes=64)
        xscale = const.tile([P, 1024], U8, name="xscale", align_bytes=64)
        nc.vector.quantize_mx(out=xcode[:].bitcast(FP8X4), scales=xscale[:], in_=xg[:])
        nc.vector.tensor_copy(out=b1col[:], in_=b1ps[:, 0:32])
        regroup_scalar(0)
        regroup_vector(0)
        regroup_scalar(1)

        hplane = {}
        hgrp = {}
        hcode = {}
        hscale = {}
        pm = {}
        acc = {}
        acc_banks = {0: (0, 1, 2, 3), 1: (4, 5, 6, 7)}
        b2bc = const.tile([P, 1024], BF16, name="b2bc")

        def first_matmul(j):
            for m in range(4):
                pm[(j, m)] = bank("pm%d_%d" % (j, m), (4 * j + m) % 8)
                for g in range(2):
                    cols = slice(512 * g + 128 * m, 512 * g + 128 * m + 128)
                    nc.tensor.matmul_mx(
                        out=pm[(j, m)][:],
                        lhsT=wcode[j][:, cols].bitcast(FP8X4),
                        lhsT_scale=wscale[j][:, cols],
                        rhs=xcode[:, 512 * g : 512 * g + 512].bitcast(FP8X4),
                        rhs_scale=xscale[:, 512 * g : 512 * g + 512],
                        start=(g == 0),
                        stop=(g == 1),
                    )

        def gelu(j):
            hplane[j] = hpool.tile([P, 4, 512], BF16, name="hp%d" % j, tag="hp")
            for m in range(4):
                nc.scalar.activation(
                    out=hplane[j][:, m, :],
                    in_=pm[(j, m)][:],
                    func=ACT.Gelu_apprx_tanh,
                    bias=b1col[:, 4 * j + m : 4 * j + m + 1],
                    scale=1.0,
                )

        def regroup_h(j):
            hgrp[j] = hpool.tile([P, 512, 4], BF16, name="hg%d" % j, tag="hg", align_bytes=64)
            nc.vector.tensor_copy(
                out=hgrp[j][:].rearrange("p (c i) t -> p c t i", i=4),
                in_=hplane[j][:].rearrange("p t (c i) -> p c t i", i=4),
            )

        def quantise_h(j):
            hcode[j] = const.tile([P, 512], U32, name="hc%d" % j, align_bytes=64)
            hscale[j] = const.tile([P, 512], U8, name="hs%d" % j, align_bytes=64)
            nc.vector.quantize_mx(
                out=hcode[j][:].bitcast(FP8X4),
                scales=hscale[j][:],
                in_=hgrp[j][:].rearrange("p w t -> p (w t)"),
            )

        def second_matmul(j, gi):
            c = (j - 8) % 4
            half = (j - 8) // 4
            g = 2 * c + gi
            for a in range(4):
                if g == 0:
                    acc[(half, a)] = bank("acc%d_%d" % (half, a), acc_banks[half][a])
                nc.tensor.matmul_mx(
                    out=acc[(half, a)][:],
                    lhsT=hcode[g][:, 128 * a : 128 * a + 128].bitcast(FP8X4),
                    lhsT_scale=hscale[g][:, 128 * a : 128 * a + 128],
                    rhs=wcode[j][:, 512 * gi : 512 * gi + 512].bitcast(FP8X4),
                    rhs_scale=wscale[j][:, 512 * gi : 512 * gi + 512],
                    start=(g == 0),
                    stop=(g == 7),
                )

        def finish(half, tiles):
            for a in tiles:
                o = outp.tile([P, 512], F32, name="o%d_%d" % (half, a), tag="osb")
                nc.vector.tensor_tensor(
                    out=o[:], in0=acc[(half, a)][:], in1=b2bc[:, 512 * half : 512 * half + 512], op=ALU.add
                )
                nc.sync.dma_start(
                    out=out[128 * a : 128 * a + 128, 512 * half : 512 * half + 512], in_=o[:]
                )

        for j in range(N_UNITS):
            if 0 <= j - 1 < 8:
                gelu(j - 1)
            if j + 2 < N_UNITS and TENSOR_COLUMNS[j + 2] > 0:
                fill_by_tensor(j + 2)
            if j == N_UNITS - 1:
                for gi in range(2):
                    quantise_unit(j, (gi,))
                    second_matmul(j, gi)
            else:
                quantise_unit(j, (0, 1))
                if j < 8:
                    first_matmul(j)
                else:
                    second_matmul(j, 0)
                    second_matmul(j, 1)
            if j in FINISH_0:
                finish(0, FINISH_0[j])
            if 0 <= j - 2 < 8:
                regroup_h(j - 2)
            if j + 2 < N_UNITS:
                regroup_scalar(j + 2)
            if j + 1 < N_UNITS:
                regroup_vector(j + 1)
            if 0 <= j - 2 < 8:
                quantise_h(j - 2)
            if j == 4:
                load_w2_chunk(3)
                nc.sync.dma_start(out=b2bc[:], in_=b2.partition_broadcast(P))
        finish(1, (0, 1, 2, 3))
